import numpy as np
import ml_dtypes


def mxq(x, axis, fmt="e4m3"):
    dtype, down = {"e4m3": (ml_dtypes.float8_e4m3fn, 7), "e5m2": (ml_dtypes.float8_e5m2, 14)}[fmt]
    v = np.moveaxis(np.asarray(x, np.float32).astype(ml_dtypes.bfloat16).astype(np.float64), axis, -1)
    blocks = v.reshape(v.shape[:-1] + (-1, 32))
    amax = np.abs(blocks).max(-1, keepdims=True)
    byte = np.maximum(np.where(amax > 0, np.frexp(amax)[1] - 1 + 127, 0) - down, 1)
    scale = np.exp2(byte - 127.0)
    codes = (blocks / scale).astype(np.float32).astype(dtype).astype(np.float64)
    return np.moveaxis((codes * scale).reshape(v.shape), -1, axis)


WIDE = False


def mx_kscale(k):
    if not WIDE:
        return np.ones(k)
    levels = np.array([10, -10, 5, -5, 0])
    a = np.random.permutation(np.resize(levels, k // 512 * 4)).reshape(k // 512, 4)
    idx = np.arange(k)
    return np.exp2(a[idx // 512, idx % 128 // 32])


BF16 = ml_dtypes.bfloat16


def bf(x):
    return np.asarray(x, np.float32).astype(BF16)


def f64(x):
    return np.asarray(x).astype(np.float64)


B, S, D, DI = 4, 512, 512, 2048
EPS = 1e-12


def l2norm(v):
    n = np.sqrt(np.sum(v * v, axis=-1, keepdims=True))
    return v / np.maximum(n, EPS)


def setup_inputs():
    s = mx_kscale(D)
    return {"x": bf(np.random.standard_normal((B, S, D)) * s),
            "wk": bf(np.random.standard_normal((D, DI)) / np.sqrt(D) / s[:, None]),
            "wv": bf(np.random.standard_normal((D, DI)) / np.sqrt(D) / s[:, None])}


def reference(x, wk, wv):
    xq = mxq(f64(x), 2, "e4m3")
    k = l2norm(xq @ mxq(f64(wk), 0, "e4m3"))
    v = xq @ mxq(f64(wv), 0, "e4m3")
    return np.sum(k * v, axis=-2, keepdims=True)

@@ -1,0 +1,231 @@
+from contextlib import ExitStack
+
+import concourse.mybir as mybir
+from concourse.masks import make_identity
+
+F32 = mybir.dt.float32
+BF16 = mybir.dt.bfloat16
+U32 = mybir.dt.uint32
+U8 = mybir.dt.uint8
+FP8X4 = mybir.dt.float8_e4m3fn_x4
+ALU = mybir.AluOpType
+ACT = mybir.ActivationFunctionType
+AXIS = mybir.AxisListType
+
+P = 128
+PACK = 4
+BATCHES = 4
+TOKENS = 512
+FEATURES = 512
+WIDTH = 2048
+EPS = 1e-12
+CHUNK = 512
+CHUNKS = WIDTH // CHUNK
+BLOCKS = WIDTH // P
+TILES_PER_BATCH = TOKENS // P
+TILES = BATCHES * TILES_PER_BATCH
+LAG = 2
+
+FLOPS = 2 * 2 * BATCHES * TOKENS * FEATURES * WIDTH
+
+
+def tile_hydraencoderlayer_pa_kernel(tc, x, wk, wv, out):
+    nc = tc.nc
+    with ExitStack() as ctx:
+        ctx.enter_context(tc.manual_schedule())
+        keep = ctx.enter_context(tc.tile_pool(name="keep", bufs=1))
+        raw_pool = ctx.enter_context(tc.tile_pool(name="raw", bufs=2 * CHUNKS))
+        grouped_pool = ctx.enter_context(tc.tile_pool(name="grouped", bufs=3))
+        key_pool = ctx.enter_context(tc.tile_pool(name="keys", bufs=LAG + 2))
+        square_pool = ctx.enter_context(tc.tile_pool(name="squares", bufs=2))
+        norm_pool = ctx.enter_context(tc.tile_pool(name="norms", bufs=LAG + 3))
+        product_pool = ctx.enter_context(tc.tile_pool(name="products", bufs=3))
+        key_banks = ctx.enter_context(tc.psum_pool(name="key_banks", bufs=4))
+        value_banks = ctx.enter_context(tc.psum_pool(name="value_banks", bufs=3))
+        sum_bank = ctx.enter_context(tc.psum_pool(name="sum_bank", bufs=1))
+
+        x_raw = keep.tile([P, BATCHES, TILES_PER_BATCH, FEATURES], BF16)
+
+        def load_x(b):
+            nc.sync.dma_start(
+                out=x_raw[:, b], in_=x[b].rearrange("(p t) k -> p t k", t=TILES_PER_BATCH)
+            )
+
+        def load_weight_chunk(w, c):
+            raw = raw_pool.tile([P, PACK, CHUNK], BF16, tag="raw")
+            for u in range(2):
+                nc.sync.dma_start(
+                    out=raw[:, 2 * u : 2 * u + 2, :],
+                    in_=w[256 * u : 256 * u + 256, c * CHUNK : (c + 1) * CHUNK].rearrange(
+                        "(p e) c -> p e c", e=2
+                    ),
+                )
+            return raw
+
+        load_x(0)
+        wk_raw = [load_weight_chunk(wk, c) for c in range(CHUNKS)]
+        load_x(1)
+        wv_raw = [load_weight_chunk(wv, c) for c in range(CHUNKS)]
+        load_x(2)
+        load_x(3)
+
+        identity = keep.tile([P, P], F32)
+        make_identity(nc, identity[:])
+        minus_half = keep.tile([P, 1], F32)
+        nc.gpsimd.memset(minus_half[:], -0.5)
+        totals = keep.tile([P, P], F32)
+        nc.vector.memset(totals[:], 0.0)
+
+        x_codes = keep.tile([P, TILES * P], U32, align_bytes=64)
+        x_scales = keep.tile([P, TILES * P], U8, align_bytes=64)
+        wk_codes = keep.tile([P, WIDTH], U32, align_bytes=64)
+        wk_scales = keep.tile([P, WIDTH], U8, align_bytes=64)
+        wv_codes = keep.tile([P, WIDTH], U32, align_bytes=64)
+        wv_scales = keep.tile([P, WIDTH], U8, align_bytes=64)
+
+        def quantise_x(b):
+            x_words = x_raw[:].bitcast(F32)
+            x_grouped = grouped_pool.tile([P, TOKENS, PACK], BF16, tag="x_grouped", bufs=2, align_bytes=64)
+            grouped_words = x_grouped[:].bitcast(F32)
+            for half in range(2):
+                flipped = key_banks.tile([P, 2, 2, P], F32, tag="bank")
+                for i in range(2):
+                    for u in range(2):
+                        nc.tensor.transpose(
+                            flipped[:, i, u, :],
+                            x_words[:, b, 2 * half + i, u * P : (u + 1) * P],
+                            identity[:],
+                        )
+                nc.vector.tensor_copy(
+                    out=grouped_words[:, 2 * half * P : 2 * (half + 1) * P, :].rearrange(
+                        "p (i k) u -> p i k u", i=2
+                    ),
+                    in_=flipped[:].rearrange("p i u k -> p i k u"),
+                )
+            columns = slice(b * TOKENS, (b + 1) * TOKENS)
+            nc.vector.quantize_mx(
+                out=x_codes[:, columns].bitcast(FP8X4),
+                scales=x_scales[:, columns],
+                in_=x_grouped[:].rearrange("p k t -> p (k t)"),
+            )
+
+        def regroup_weight_chunk(raw):
+            grouped = grouped_pool.tile([P, CHUNK, PACK], BF16, tag="w_grouped", align_bytes=64)
+            nc.vector.tensor_copy(
+                out=grouped[:].rearrange("p (c i) t -> p c t i", i=4),
+                in_=raw[:].rearrange("p t (c i) -> p c t i", i=4),
+            )
+            return grouped
+
+        def quantise_weight_chunk(grouped, codes, scales, c):
+            columns = slice(c * CHUNK, (c + 1) * CHUNK)
+            nc.vector.quantize_mx(
+                out=codes[:, columns].bitcast(FP8X4),
+                scales=scales[:, columns],
+                in_=grouped[:].rearrange("p c t -> p (c t)"),
+            )
+
+        def quantise_weight(raws, codes, scales, first, count):
+            grouped = [None] * CHUNKS
+            for c in range(first, first + count + 1):
+                if c < first + count:
+                    grouped[c] = regroup_weight_chunk(raws[c])
+                if c > first:
+                    quantise_weight_chunk(grouped[c - 1], codes, scales, c - 1)
+
+        sums = sum_bank.tile([P, TILES * BLOCKS], F32)
+        keys = [None] * TILES
+        inverse_norms = [None] * TILES
+        weighted = [None] * TILES
+
+        def key_stage(t):
+            tokens = slice(t * P, (t + 1) * P)
+            a_sb = key_pool.tile([P, WIDTH], F32, tag="a_sb")
+            for c in range(CHUNKS):
+                columns = slice(c * CHUNK, (c + 1) * CHUNK)
+                a_bank = key_banks.tile([P, CHUNK], F32, tag="bank")
+                nc.tensor.matmul_mx(
+                    out=a_bank[:],
+                    lhsT=x_codes[:, tokens].bitcast(FP8X4),
+                    lhsT_scale=x_scales[:, tokens],
+                    rhs=wk_codes[:, columns].bitcast(FP8X4),
+                    rhs_scale=wk_scales[:, columns],
+                    start=True,
+                    stop=True,
+                )
+                if c == 0:
+                    nc.vector.tensor_copy(out=a_sb[:, columns], in_=a_bank[:])
+                else:
+                    nc.scalar.copy(out=a_sb[:, columns], in_=a_bank[:])
+            squares = square_pool.tile([P, WIDTH], BF16, tag="squares")
+            norm_squared = norm_pool.tile([P, 1], F32, tag="norm_squared")
+            nc.scalar.activation(
+                out=squares[:], in_=a_sb[:], func=ACT.Square, accum_out=norm_squared[:]
+            )
+            clamped = norm_pool.tile([P, 1], F32, tag="clamped")
+            nc.gpsimd.tensor_scalar_max(out=clamped[:], in0=norm_squared[:], scalar1=EPS * EPS)
+            inverse_norm = norm_pool.tile([P, 1], F32, tag="inverse_norm")
+            nc.gpsimd.tensor_tensor(
+                out=inverse_norm[:], in0=clamped[:], in1=minus_half[:], op=ALU.pow
+            )
+            keys[t] = a_sb
+            inverse_norms[t] = inverse_norm
+
+        def value_stage(t):
+            tokens = slice(t * P, (t + 1) * P)
+            products = product_pool.tile([P, WIDTH], F32, tag="products")
+            for c in range(CHUNKS):
+                columns = slice(c * CHUNK, (c + 1) * CHUNK)
+                v_bank = value_banks.tile([P, CHUNK], F32, tag="bank")
+                nc.tensor.matmul_mx(
+                    out=v_bank[:],
+                    lhsT=x_codes[:, tokens].bitcast(FP8X4),
+                    lhsT_scale=x_scales[:, tokens],
+                    rhs=wv_codes[:, columns].bitcast(FP8X4),
+                    rhs_scale=wv_scales[:, columns],
+                    start=True,
+                    stop=True,
+                )
+                nc.vector.tensor_tensor(
+                    out=products[:, columns], in0=v_bank[:], in1=keys[t][:, columns], op=ALU.mult
+                )
+            weighted[t] = products
+
+        def sum_stage(t):
+            for j in range(BLOCKS):
+                nc.tensor.matmul(
+                    out=sums[:, t * BLOCKS + j : t * BLOCKS + j + 1],
+                    lhsT=weighted[t][:, j * P : (j + 1) * P],
+                    rhs=inverse_norms[t][:],
+                    start=True,
+                    stop=True,
+                )
+
+        quantise_x(0)
+        quantise_weight(wk_raw, wk_codes, wk_scales, 0, CHUNKS)
+        for t in range(TILES + LAG + 1):
+            if t < TILES:
+                key_stage(t)
+                if t % TILES_PER_BATCH == 0 and t // TILES_PER_BATCH + 1 < BATCHES:
+                    quantise_x(t // TILES_PER_BATCH + 1)
+            if t < LAG:
+                quantise_weight(wv_raw, wv_codes, wv_scales, t * (CHUNKS // LAG), CHUNKS // LAG)
+            if LAG <= t < TILES + LAG:
+                value_stage(t - LAG)
+            if t > LAG:
+                sum_stage(t - LAG - 1)
+
+        nc.vector.tensor_reduce(
+            out=totals[:, 0 : BATCHES * BLOCKS].rearrange("p (b j) -> p b j", b=BATCHES),
+            in_=sums[:].rearrange("p (b t j) -> p b j t", b=BATCHES, t=TILES_PER_BATCH),
+            axis=AXIS.X,
+            op=ALU.add,
+        )
+        turned = key_banks.tile([P, P], F32, tag="bank")
+        nc.tensor.transpose(turned[:], totals[:], identity[:])
+        result = keep.tile([P, P], F32)
+        nc.vector.tensor_copy(out=result[:], in_=turned[:])
+        nc.sync.dma_start(
+            out=out.rearrange("b o (j l) -> (b o j) l", l=P),
+            in_=result[0 : BATCHES * BLOCKS, :],
+        )

@@ -10,7 +10,6 @@ U8 = mybir.dt.uint8
 FP8X4 = mybir.dt.float8_e4m3fn_x4
 ALU = mybir.AluOpType
 ACT = mybir.ActivationFunctionType
-AXIS = mybir.AxisListType
 
 P = 128
 PACK = 4
@@ -21,10 +20,10 @@ WIDTH = 2048
 EPS = 1e-12
 CHUNK = 512
 CHUNKS = WIDTH // CHUNK
-BLOCKS = WIDTH // P
 TILES_PER_BATCH = TOKENS // P
 TILES = BATCHES * TILES_PER_BATCH
-LAG = 2
+VALUE_LAG = 2
+SUM_LAG = TILES_PER_BATCH
 
 FLOPS = 2 * 2 * BATCHES * TOKENS * FEATURES * WIDTH
 
@@ -36,13 +35,14 @@ def tile_hydraencoderlayer_pa_kernel(tc, x, wk, wv, out):
         keep = ctx.enter_context(tc.tile_pool(name="keep", bufs=1))
         raw_pool = ctx.enter_context(tc.tile_pool(name="raw", bufs=2 * CHUNKS))
         grouped_pool = ctx.enter_context(tc.tile_pool(name="grouped", bufs=3))
-        key_pool = ctx.enter_context(tc.tile_pool(name="keys", bufs=LAG + 2))
+        key_pool = ctx.enter_context(tc.tile_pool(name="keys", bufs=VALUE_LAG + 2))
         square_pool = ctx.enter_context(tc.tile_pool(name="squares", bufs=2))
-        norm_pool = ctx.enter_context(tc.tile_pool(name="norms", bufs=LAG + 3))
-        product_pool = ctx.enter_context(tc.tile_pool(name="products", bufs=3))
+        norm_pool = ctx.enter_context(tc.tile_pool(name="norms", bufs=VALUE_LAG + 2))
+        product_pool = ctx.enter_context(tc.tile_pool(name="products", bufs=2 * CHUNKS))
+        batch_pool = ctx.enter_context(tc.tile_pool(name="batch_sums", bufs=2))
         key_banks = ctx.enter_context(tc.psum_pool(name="key_banks", bufs=4))
         value_banks = ctx.enter_context(tc.psum_pool(name="value_banks", bufs=3))
-        sum_bank = ctx.enter_context(tc.psum_pool(name="sum_bank", bufs=1))
+        total_bank = ctx.enter_context(tc.psum_pool(name="total_bank", bufs=1))
 
         x_raw = keep.tile([P, BATCHES, TILES_PER_BATCH, FEATURES], BF16)
 
@@ -71,10 +71,12 @@ def tile_hydraencoderlayer_pa_kernel(tc, x, wk, wv, out):
 
         identity = keep.tile([P, P], F32)
         make_identity(nc, identity[:])
-        minus_half = keep.tile([P, 1], F32)
-        nc.gpsimd.memset(minus_half[:], -0.5)
-        totals = keep.tile([P, P], F32)
-        nc.vector.memset(totals[:], 0.0)
+        selector = keep.tile([P, 2 * P], F32)
+        nc.vector.memset(selector[:], 0.0)
+        nc.vector.memset(selector[:, P - 1 : P], 1.0)
+        one = keep.tile([P, 1], F32)
+        nc.vector.memset(one[:], 1.0)
+        nc.scalar.sqrt(out=one[:], in_=one[:])
 
         x_codes = keep.tile([P, TILES * P], U32, align_bytes=64)
         x_scales = keep.tile([P, TILES * P], U8, align_bytes=64)
@@ -85,7 +87,9 @@ def tile_hydraencoderlayer_pa_kernel(tc, x, wk, wv, out):
 
         def quantise_x(b):
             x_words = x_raw[:].bitcast(F32)
-            x_grouped = grouped_pool.tile([P, TOKENS, PACK], BF16, tag="x_grouped", bufs=2, align_bytes=64)
+            x_grouped = grouped_pool.tile(
+                [P, TOKENS, PACK], BF16, tag="x_grouped", bufs=2, align_bytes=64
+            )
             grouped_words = x_grouped[:].bitcast(F32)
             for half in range(2):
                 flipped = key_banks.tile([P, 2, 2, P], F32, tag="bank")
@@ -133,14 +137,16 @@ def tile_hydraencoderlayer_pa_kernel(tc, x, wk, wv, out):
                 if c > first:
                     quantise_weight_chunk(grouped[c - 1], codes, scales, c - 1)
 
-        sums = sum_bank.tile([P, TILES * BLOCKS], F32)
+        totals = total_bank.tile([P, CHUNK], F32)
         keys = [None] * TILES
+        norms_squared = [None] * TILES
+        norms = [None] * TILES
         inverse_norms = [None] * TILES
-        weighted = [None] * TILES
+        batch_sums = [None] * BATCHES
 
-        def key_stage(t):
+        def key_products(t):
             tokens = slice(t * P, (t + 1) * P)
-            a_sb = key_pool.tile([P, WIDTH], F32, tag="a_sb")
+            keys[t] = key_pool.tile([P, WIDTH], F32, name="a_sb", tag="a_sb")
             for c in range(CHUNKS):
                 columns = slice(c * CHUNK, (c + 1) * CHUNK)
                 a_bank = key_banks.tile([P, CHUNK], F32, tag="bank")
@@ -154,26 +160,33 @@ def tile_hydraencoderlayer_pa_kernel(tc, x, wk, wv, out):
                     stop=True,
                 )
                 if c == 0:
-                    nc.vector.tensor_copy(out=a_sb[:, columns], in_=a_bank[:])
+                    nc.vector.tensor_copy(out=keys[t][:, columns], in_=a_bank[:])
                 else:
-                    nc.scalar.copy(out=a_sb[:, columns], in_=a_bank[:])
+                    nc.scalar.copy(out=keys[t][:, columns], in_=a_bank[:])
+
+        def sum_of_squares(t):
             squares = square_pool.tile([P, WIDTH], BF16, tag="squares")
-            norm_squared = norm_pool.tile([P, 1], F32, tag="norm_squared")
+            norms_squared[t] = norm_pool.tile([P, 1], F32, name="norm_squared", tag="norm_squared")
             nc.scalar.activation(
-                out=squares[:], in_=a_sb[:], func=ACT.Square, accum_out=norm_squared[:]
+                out=squares[:], in_=keys[t][:], func=ACT.Square, accum_out=norms_squared[t][:]
             )
+
+        def clamp_and_root(t):
             clamped = norm_pool.tile([P, 1], F32, tag="clamped")
-            nc.gpsimd.tensor_scalar_max(out=clamped[:], in0=norm_squared[:], scalar1=EPS * EPS)
-            inverse_norm = norm_pool.tile([P, 1], F32, tag="inverse_norm")
-            nc.gpsimd.tensor_tensor(
-                out=inverse_norm[:], in0=clamped[:], in1=minus_half[:], op=ALU.pow
-            )
-            keys[t] = a_sb
-            inverse_norms[t] = inverse_norm
+            nc.vector.tensor_scalar_max(out=clamped[:], in0=norms_squared[t][:], scalar1=EPS * EPS)
+            norms[t] = norm_pool.tile([P, 1], F32, name="norm", tag="norm")
+            nc.scalar.sqrt(out=norms[t][:], in_=clamped[:])
+
+        def invert_norm(t):
+            inverse_norms[t] = norm_pool.tile([P, 1], F32, name="inverse_norm", tag="inverse_norm")
+            nc.vector.reciprocal(out=inverse_norms[t][:], in_=norms[t][:])
 
         def value_stage(t):
+            b = t // TILES_PER_BATCH
+            first_of_batch = t % TILES_PER_BATCH == 0
             tokens = slice(t * P, (t + 1) * P)
-            products = product_pool.tile([P, WIDTH], F32, tag="products")
+            if first_of_batch:
+                batch_sums[b] = batch_pool.tile([P, WIDTH], F32, name="batch_sum", tag="batch_sum")
             for c in range(CHUNKS):
                 columns = slice(c * CHUNK, (c + 1) * CHUNK)
                 v_bank = value_banks.tile([P, CHUNK], F32, tag="bank")
@@ -186,46 +199,64 @@ def tile_hydraencoderlayer_pa_kernel(tc, x, wk, wv, out):
                     start=True,
                     stop=True,
                 )
-                nc.vector.tensor_tensor(
-                    out=products[:, columns], in0=v_bank[:], in1=keys[t][:, columns], op=ALU.mult
+                if first_of_batch:
+                    product = batch_sums[b][:, columns]
+                else:
+                    product_tile = product_pool.tile([P, CHUNK], F32, tag="product")
+                    product = product_tile[:]
+                nc.vector.scalar_tensor_tensor(
+                    out=product,
+                    in0=v_bank[:],
+                    scalar=inverse_norms[t][:],
+                    in1=keys[t][:, columns],
+                    op0=ALU.mult,
+                    op1=ALU.mult,
                 )
-            weighted[t] = products
+                if not first_of_batch:
+                    nc.gpsimd.tensor_tensor(
+                        out=batch_sums[b][:, columns],
+                        in0=batch_sums[b][:, columns],
+                        in1=product,
+                        op=ALU.add,
+                    )
 
-        def sum_stage(t):
-            for j in range(BLOCKS):
-                nc.tensor.matmul(
-                    out=sums[:, t * BLOCKS + j : t * BLOCKS + j + 1],
-                    lhsT=weighted[t][:, j * P : (j + 1) * P],
-                    rhs=inverse_norms[t][:],
-                    start=True,
-                    stop=True,
-                )
+        def sum_over_partitions(m):
+            b, c = divmod(m, CHUNKS)
+            nc.tensor.matmul(
+                out=totals[:],
+                lhsT=selector[:, P - 1 - m : 2 * P - 1 - m],
+                rhs=batch_sums[b][:, c * CHUNK : (c + 1) * CHUNK],
+                start=(m == 0),
+                stop=(m == BATCHES * CHUNKS - 1),
+            )
+
+        def is_tile(t):
+            return 0 <= t < TILES
 
         quantise_x(0)
         quantise_weight(wk_raw, wk_codes, wk_scales, 0, CHUNKS)
-        for t in range(TILES + LAG + 1):
-            if t < TILES:
-                key_stage(t)
-                if t % TILES_PER_BATCH == 0 and t // TILES_PER_BATCH + 1 < BATCHES:
-                    quantise_x(t // TILES_PER_BATCH + 1)
-            if t < LAG:
-                quantise_weight(wv_raw, wv_codes, wv_scales, t * (CHUNKS // LAG), CHUNKS // LAG)
-            if LAG <= t < TILES + LAG:
-                value_stage(t - LAG)
-            if t > LAG:
-                sum_stage(t - LAG - 1)
+        for t in range(TILES + VALUE_LAG + SUM_LAG):
+            if is_tile(t):
+                key_products(t)
+            if is_tile(t - 1):
+                clamp_and_root(t - 1)
+            if is_tile(t):
+                sum_of_squares(t)
+            if t < VALUE_LAG:
+                share = CHUNKS // VALUE_LAG
+                quantise_weight(wv_raw, wv_codes, wv_scales, t * share, share)
+            if is_tile(t - VALUE_LAG):
+                value_stage(t - VALUE_LAG)
+            if is_tile(t - 1):
+                invert_norm(t - 1)
+            if is_tile(t) and t % TILES_PER_BATCH == 2 and t // TILES_PER_BATCH + 1 < BATCHES:
+                quantise_x(t // TILES_PER_BATCH + 1)
+            if is_tile(t - VALUE_LAG - SUM_LAG):
+                sum_over_partitions(t - VALUE_LAG - SUM_LAG)
 
-        nc.vector.tensor_reduce(
-            out=totals[:, 0 : BATCHES * BLOCKS].rearrange("p (b j) -> p b j", b=BATCHES),
-            in_=sums[:].rearrange("p (b t j) -> p b j t", b=BATCHES, t=TILES_PER_BATCH),
-            axis=AXIS.X,
-            op=ALU.add,
-        )
-        turned = key_banks.tile([P, P], F32, tag="bank")
-        nc.tensor.transpose(turned[:], totals[:], identity[:])
-        result = keep.tile([P, P], F32)
-        nc.vector.tensor_copy(out=result[:], in_=turned[:])
+        rows = BATCHES * CHUNKS
+        result = keep.tile([P, CHUNK], F32)
+        nc.scalar.copy(out=result[0:rows, :], in_=totals[0:rows, :])
         nc.sync.dma_start(
-            out=out.rearrange("b o (j l) -> (b o j) l", l=P),
-            in_=result[0 : BATCHES * BLOCKS, :],
+            out=out.rearrange("b o (c n) -> (b o c) n", n=CHUNK), in_=result[0:rows, :]
         )

@@ -20,10 +20,11 @@ WIDTH = 2048
 EPS = 1e-12
 CHUNK = 512
 CHUNKS = WIDTH // CHUNK
-TILES_PER_BATCH = TOKENS // P
-TILES = BATCHES * TILES_PER_BATCH
+TILES = BATCHES * TOKENS // P
+LANES = P // BATCHES
+GROUP = 4
+GROUPS = TILES // GROUP
 VALUE_LAG = 2
-SUM_LAG = TILES_PER_BATCH
 
 FLOPS = 2 * 2 * BATCHES * TOKENS * FEATURES * WIDTH
 
@@ -39,17 +40,14 @@ def tile_hydraencoderlayer_pa_kernel(tc, x, wk, wv, out):
         square_pool = ctx.enter_context(tc.tile_pool(name="squares", bufs=2))
         norm_pool = ctx.enter_context(tc.tile_pool(name="norms", bufs=VALUE_LAG + 2))
         product_pool = ctx.enter_context(tc.tile_pool(name="products", bufs=2 * CHUNKS))
-        batch_pool = ctx.enter_context(tc.tile_pool(name="batch_sums", bufs=2))
         key_banks = ctx.enter_context(tc.psum_pool(name="key_banks", bufs=4))
-        value_banks = ctx.enter_context(tc.psum_pool(name="value_banks", bufs=3))
-        total_bank = ctx.enter_context(tc.psum_pool(name="total_bank", bufs=1))
+        value_banks = ctx.enter_context(tc.psum_pool(name="value_banks", bufs=4))
 
-        x_raw = keep.tile([P, BATCHES, TILES_PER_BATCH, FEATURES], BF16)
+        x_raw = keep.tile([P, GROUPS, GROUP, FEATURES], BF16)
+        x_tiles = x.rearrange("b (q t) k -> (b q) t k", t=TILES)
 
-        def load_x(b):
-            nc.sync.dma_start(
-                out=x_raw[:, b], in_=x[b].rearrange("(p t) k -> p t k", t=TILES_PER_BATCH)
-            )
+        def load_x(g):
+            nc.sync.dma_start(out=x_raw[:, g], in_=x_tiles[:, g * GROUP : (g + 1) * GROUP, :])
 
         def load_weight_chunk(w, c):
             raw = raw_pool.tile([P, PACK, CHUNK], BF16, tag="raw")
@@ -71,9 +69,11 @@ def tile_hydraencoderlayer_pa_kernel(tc, x, wk, wv, out):
 
         identity = keep.tile([P, P], F32)
         make_identity(nc, identity[:])
-        selector = keep.tile([P, 2 * P], F32)
+        selector = keep.tile([P, P + CHUNKS - 1], F32)
         nc.vector.memset(selector[:], 0.0)
-        nc.vector.memset(selector[:, P - 1 : P], 1.0)
+        for b in range(BATCHES):
+            column = CHUNKS - 1 + CHUNKS * b
+            nc.vector.memset(selector[b * LANES : (b + 1) * LANES, column : column + 1], 1.0)
         one = keep.tile([P, 1], F32)
         nc.vector.memset(one[:], 1.0)
         nc.scalar.sqrt(out=one[:], in_=one[:])
@@ -85,10 +85,10 @@ def tile_hydraencoderlayer_pa_kernel(tc, x, wk, wv, out):
         wv_codes = keep.tile([P, WIDTH], U32, align_bytes=64)
         wv_scales = keep.tile([P, WIDTH], U8, align_bytes=64)
 
-        def quantise_x(b):
+        def quantise_x(g):
             x_words = x_raw[:].bitcast(F32)
             x_grouped = grouped_pool.tile(
-                [P, TOKENS, PACK], BF16, tag="x_grouped", bufs=2, align_bytes=64
+                [P, GROUP * P, PACK], BF16, tag="x_grouped", bufs=2, align_bytes=64
             )
             grouped_words = x_grouped[:].bitcast(F32)
             for half in range(2):
@@ -97,7 +97,7 @@ def tile_hydraencoderlayer_pa_kernel(tc, x, wk, wv, out):
                     for u in range(2):
                         nc.tensor.transpose(
                             flipped[:, i, u, :],
-                            x_words[:, b, 2 * half + i, u * P : (u + 1) * P],
+                            x_words[:, g, 2 * half + i, u * P : (u + 1) * P],
                             identity[:],
                         )
                 nc.vector.tensor_copy(
@@ -106,7 +106,7 @@ def tile_hydraencoderlayer_pa_kernel(tc, x, wk, wv, out):
                     ),
                     in_=flipped[:].rearrange("p i u k -> p i k u"),
                 )
-            columns = slice(b * TOKENS, (b + 1) * TOKENS)
+            columns = slice(g * GROUP * P, (g + 1) * GROUP * P)
             nc.vector.quantize_mx(
                 out=x_codes[:, columns].bitcast(FP8X4),
                 scales=x_scales[:, columns],
@@ -137,12 +137,11 @@ def tile_hydraencoderlayer_pa_kernel(tc, x, wk, wv, out):
                 if c > first:
                     quantise_weight_chunk(grouped[c - 1], codes, scales, c - 1)
 
-        totals = total_bank.tile([P, CHUNK], F32)
+        lane_sums = keep.tile([P, WIDTH], F32)
         keys = [None] * TILES
         norms_squared = [None] * TILES
         norms = [None] * TILES
         inverse_norms = [None] * TILES
-        batch_sums = [None] * BATCHES
 
         def key_products(t):
             tokens = slice(t * P, (t + 1) * P)
@@ -181,12 +180,15 @@ def tile_hydraencoderlayer_pa_kernel(tc, x, wk, wv, out):
             inverse_norms[t] = norm_pool.tile([P, 1], F32, name="inverse_norm", tag="inverse_norm")
             nc.vector.reciprocal(out=inverse_norms[t][:], in_=norms[t][:])
 
+        def add_to_lane_sums(engine, c, product):
+            columns = slice(c * CHUNK, (c + 1) * CHUNK)
+            engine.tensor_tensor(
+                out=lane_sums[:, columns], in0=lane_sums[:, columns], in1=product, op=ALU.add
+            )
+
         def value_stage(t):
-            b = t // TILES_PER_BATCH
-            first_of_batch = t % TILES_PER_BATCH == 0
             tokens = slice(t * P, (t + 1) * P)
-            if first_of_batch:
-                batch_sums[b] = batch_pool.tile([P, WIDTH], F32, name="batch_sum", tag="batch_sum")
+            products = [None] * CHUNKS
             for c in range(CHUNKS):
                 columns = slice(c * CHUNK, (c + 1) * CHUNK)
                 v_bank = value_banks.tile([P, CHUNK], F32, tag="bank")
@@ -199,43 +201,30 @@ def tile_hydraencoderlayer_pa_kernel(tc, x, wk, wv, out):
                     start=True,
                     stop=True,
                 )
-                if first_of_batch:
-                    product = batch_sums[b][:, columns]
+                if t == 0:
+                    products[c] = lane_sums[:, columns]
                 else:
                     product_tile = product_pool.tile([P, CHUNK], F32, tag="product")
-                    product = product_tile[:]
+                    products[c] = product_tile[:]
                 nc.vector.scalar_tensor_tensor(
-                    out=product,
+                    out=products[c],
                     in0=v_bank[:],
                     scalar=inverse_norms[t][:],
                     in1=keys[t][:, columns],
                     op0=ALU.mult,
                     op1=ALU.mult,
                 )
-                if not first_of_batch:
-                    nc.gpsimd.tensor_tensor(
-                        out=batch_sums[b][:, columns],
-                        in0=batch_sums[b][:, columns],
-                        in1=product,
-                        op=ALU.add,
-                    )
-
-        def sum_over_partitions(m):
-            b, c = divmod(m, CHUNKS)
-            nc.tensor.matmul(
-                out=totals[:],
-                lhsT=selector[:, P - 1 - m : 2 * P - 1 - m],
-                rhs=batch_sums[b][:, c * CHUNK : (c + 1) * CHUNK],
-                start=(m == 0),
-                stop=(m == BATCHES * CHUNKS - 1),
-            )
+                if t > 0 and c == 1:
+                    add_to_lane_sums(nc.vector, 0, products[0])
+                if t > 0 and c >= 1:
+                    add_to_lane_sums(nc.gpsimd, c, products[c])
 
         def is_tile(t):
             return 0 <= t < TILES
 
         quantise_x(0)
         quantise_weight(wk_raw, wk_codes, wk_scales, 0, CHUNKS)
-        for t in range(TILES + VALUE_LAG + SUM_LAG):
+        for t in range(TILES + VALUE_LAG):
             if is_tile(t):
                 key_products(t)
             if is_tile(t - 1):
@@ -249,11 +238,18 @@ def tile_hydraencoderlayer_pa_kernel(tc, x, wk, wv, out):
                 value_stage(t - VALUE_LAG)
             if is_tile(t - 1):
                 invert_norm(t - 1)
-            if is_tile(t) and t % TILES_PER_BATCH == 2 and t // TILES_PER_BATCH + 1 < BATCHES:
-                quantise_x(t // TILES_PER_BATCH + 1)
-            if is_tile(t - VALUE_LAG - SUM_LAG):
-                sum_over_partitions(t - VALUE_LAG - SUM_LAG)
+            if t % GROUP == GROUP - 2 and t // GROUP + 1 < GROUPS:
+                quantise_x(t // GROUP + 1)
 
+        totals = key_banks.tile([P, CHUNK], F32, tag="bank")
+        for c in range(CHUNKS):
+            nc.tensor.matmul(
+                out=totals[:],
+                lhsT=selector[:, CHUNKS - 1 - c : CHUNKS - 1 - c + P],
+                rhs=lane_sums[:, c * CHUNK : (c + 1) * CHUNK],
+                start=(c == 0),
+                stop=(c == CHUNKS - 1),
+            )
         rows = BATCHES * CHUNKS
         result = keep.tile([P, CHUNK], F32)
         nc.scalar.copy(out=result[0:rows, :], in_=totals[0:rows, :])

@@ -10,6 +10,7 @@ U8 = mybir.dt.uint8
 FP8X4 = mybir.dt.float8_e4m3fn_x4
 ALU = mybir.AluOpType
 ACT = mybir.ActivationFunctionType
+AXIS = mybir.AxisListType
 
 P = 128
 PACK = 4
@@ -20,11 +21,11 @@ WIDTH = 2048
 EPS = 1e-12
 CHUNK = 512
 CHUNKS = WIDTH // CHUNK
-TILES = BATCHES * TOKENS // P
-LANES = P // BATCHES
-GROUP = 4
-GROUPS = TILES // GROUP
+BLOCKS = CHUNK // P
+TILES_PER_BATCH = TOKENS // P
+TILES = BATCHES * TILES_PER_BATCH
 VALUE_LAG = 2
+SUM_LAG = TILES_PER_BATCH
 
 FLOPS = 2 * 2 * BATCHES * TOKENS * FEATURES * WIDTH
 
@@ -35,19 +36,21 @@ def tile_hydraencoderlayer_pa_kernel(tc, x, wk, wv, out):
         ctx.enter_context(tc.manual_schedule())
         keep = ctx.enter_context(tc.tile_pool(name="keep", bufs=1))
         raw_pool = ctx.enter_context(tc.tile_pool(name="raw", bufs=2 * CHUNKS))
-        grouped_pool = ctx.enter_context(tc.tile_pool(name="grouped", bufs=3))
+        grouped_pool = ctx.enter_context(tc.tile_pool(name="grouped", bufs=4))
         key_pool = ctx.enter_context(tc.tile_pool(name="keys", bufs=VALUE_LAG + 2))
         square_pool = ctx.enter_context(tc.tile_pool(name="squares", bufs=2))
         norm_pool = ctx.enter_context(tc.tile_pool(name="norms", bufs=VALUE_LAG + 2))
         product_pool = ctx.enter_context(tc.tile_pool(name="products", bufs=2 * CHUNKS))
+        batch_pool = ctx.enter_context(tc.tile_pool(name="batch_sums", bufs=2))
         key_banks = ctx.enter_context(tc.psum_pool(name="key_banks", bufs=4))
         value_banks = ctx.enter_context(tc.psum_pool(name="value_banks", bufs=4))
 
-        x_raw = keep.tile([P, GROUPS, GROUP, FEATURES], BF16)
-        x_tiles = x.rearrange("b (q t) k -> (b q) t k", t=TILES)
+        x_raw = keep.tile([P, BATCHES, TILES_PER_BATCH, FEATURES], BF16)
 
-        def load_x(g):
-            nc.sync.dma_start(out=x_raw[:, g], in_=x_tiles[:, g * GROUP : (g + 1) * GROUP, :])
+        def load_x(b):
+            nc.sync.dma_start(
+                out=x_raw[:, b], in_=x[b].rearrange("(p t) k -> p t k", t=TILES_PER_BATCH)
+            )
 
         def load_weight_chunk(w, c):
             raw = raw_pool.tile([P, PACK, CHUNK], BF16, tag="raw")
@@ -69,11 +72,8 @@ def tile_hydraencoderlayer_pa_kernel(tc, x, wk, wv, out):
 
         identity = keep.tile([P, P], F32)
         make_identity(nc, identity[:])
-        selector = keep.tile([P, P + CHUNKS - 1], F32)
-        nc.vector.memset(selector[:], 0.0)
-        for b in range(BATCHES):
-            column = CHUNKS - 1 + CHUNKS * b
-            nc.vector.memset(selector[b * LANES : (b + 1) * LANES, column : column + 1], 1.0)
+        sums = keep.tile([P, P], F32)
+        nc.vector.memset(sums[:], 0.0)
         one = keep.tile([P, 1], F32)
         nc.vector.memset(one[:], 1.0)
         nc.scalar.sqrt(out=one[:], in_=one[:])
@@ -85,10 +85,10 @@ def tile_hydraencoderlayer_pa_kernel(tc, x, wk, wv, out):
         wv_codes = keep.tile([P, WIDTH], U32, align_bytes=64)
         wv_scales = keep.tile([P, WIDTH], U8, align_bytes=64)
 
-        def quantise_x(g):
+        def quantise_x(b):
             x_words = x_raw[:].bitcast(F32)
             x_grouped = grouped_pool.tile(
-                [P, GROUP * P, PACK], BF16, tag="x_grouped", bufs=2, align_bytes=64
+                [P, TOKENS, PACK], BF16, tag="x_grouped", bufs=2, align_bytes=64
             )
             grouped_words = x_grouped[:].bitcast(F32)
             for half in range(2):
@@ -97,7 +97,7 @@ def tile_hydraencoderlayer_pa_kernel(tc, x, wk, wv, out):
                     for u in range(2):
                         nc.tensor.transpose(
                             flipped[:, i, u, :],
-                            x_words[:, g, 2 * half + i, u * P : (u + 1) * P],
+                            x_words[:, b, 2 * half + i, u * P : (u + 1) * P],
                             identity[:],
                         )
                 nc.vector.tensor_copy(
@@ -106,16 +106,16 @@ def tile_hydraencoderlayer_pa_kernel(tc, x, wk, wv, out):
                     ),
                     in_=flipped[:].rearrange("p i u k -> p i k u"),
                 )
-            columns = slice(g * GROUP * P, (g + 1) * GROUP * P)
+            columns = slice(b * TOKENS, (b + 1) * TOKENS)
             nc.vector.quantize_mx(
                 out=x_codes[:, columns].bitcast(FP8X4),
                 scales=x_scales[:, columns],
                 in_=x_grouped[:].rearrange("p k t -> p (k t)"),
             )
 
-        def regroup_weight_chunk(raw):
+        def regroup_weight_chunk(raw, copy):
             grouped = grouped_pool.tile([P, CHUNK, PACK], BF16, tag="w_grouped", align_bytes=64)
-            nc.vector.tensor_copy(
+            copy(
                 out=grouped[:].rearrange("p (c i) t -> p c t i", i=4),
                 in_=raw[:].rearrange("p t (c i) -> p c t i", i=4),
             )
@@ -129,19 +129,21 @@ def tile_hydraencoderlayer_pa_kernel(tc, x, wk, wv, out):
                 in_=grouped[:].rearrange("p c t -> p (c t)"),
             )
 
-        def quantise_weight(raws, codes, scales, first, count):
+        def quantise_weight(raws, codes, scales, first, count, odd_copy):
             grouped = [None] * CHUNKS
             for c in range(first, first + count + 1):
                 if c < first + count:
-                    grouped[c] = regroup_weight_chunk(raws[c])
+                    copy = odd_copy if c % 2 == 1 else nc.vector.tensor_copy
+                    grouped[c] = regroup_weight_chunk(raws[c], copy)
                 if c > first:
                     quantise_weight_chunk(grouped[c - 1], codes, scales, c - 1)
 
-        lane_sums = keep.tile([P, WIDTH], F32)
         keys = [None] * TILES
         norms_squared = [None] * TILES
         norms = [None] * TILES
         inverse_norms = [None] * TILES
+        first_three = [None] * BATCHES
+        fourth = [None] * BATCHES
 
         def key_products(t):
             tokens = slice(t * P, (t + 1) * P)
@@ -180,15 +182,13 @@ def tile_hydraencoderlayer_pa_kernel(tc, x, wk, wv, out):
             inverse_norms[t] = norm_pool.tile([P, 1], F32, name="inverse_norm", tag="inverse_norm")
             nc.vector.reciprocal(out=inverse_norms[t][:], in_=norms[t][:])
 
-        def add_to_lane_sums(engine, c, product):
-            columns = slice(c * CHUNK, (c + 1) * CHUNK)
-            engine.tensor_tensor(
-                out=lane_sums[:, columns], in0=lane_sums[:, columns], in1=product, op=ALU.add
-            )
-
         def value_stage(t):
+            b, place = divmod(t, TILES_PER_BATCH)
             tokens = slice(t * P, (t + 1) * P)
-            products = [None] * CHUNKS
+            if place == 0:
+                first_three[b] = batch_pool.tile([P, WIDTH], F32, name="first_three", tag="first_three")
+            if place == TILES_PER_BATCH - 1:
+                fourth[b] = batch_pool.tile([P, WIDTH], F32, name="fourth", tag="fourth")
             for c in range(CHUNKS):
                 columns = slice(c * CHUNK, (c + 1) * CHUNK)
                 v_bank = value_banks.tile([P, CHUNK], F32, tag="bank")
@@ -201,30 +201,60 @@ def tile_hydraencoderlayer_pa_kernel(tc, x, wk, wv, out):
                     start=True,
                     stop=True,
                 )
-                if t == 0:
-                    products[c] = lane_sums[:, columns]
+                if place == 0:
+                    product = first_three[b][:, columns]
+                elif place == TILES_PER_BATCH - 1:
+                    product = fourth[b][:, columns]
                 else:
                     product_tile = product_pool.tile([P, CHUNK], F32, tag="product")
-                    products[c] = product_tile[:]
+                    product = product_tile[:]
                 nc.vector.scalar_tensor_tensor(
-                    out=products[c],
+                    out=product,
                     in0=v_bank[:],
                     scalar=inverse_norms[t][:],
                     in1=keys[t][:, columns],
                     op0=ALU.mult,
                     op1=ALU.mult,
                 )
-                if t > 0 and c == 1:
-                    add_to_lane_sums(nc.vector, 0, products[0])
-                if t > 0 and c >= 1:
-                    add_to_lane_sums(nc.gpsimd, c, products[c])
+                if 0 < place < TILES_PER_BATCH - 1:
+                    nc.gpsimd.tensor_tensor(
+                        out=first_three[b][:, columns],
+                        in0=first_three[b][:, columns],
+                        in1=product,
+                        op=ALU.add,
+                    )
+
+        def sum_over_tokens(m):
+            b, c = divmod(m, CHUNKS)
+            turned = value_banks.tile([P, BLOCKS, P], F32, tag="bank")
+            for j in range(BLOCKS):
+                block = slice(c * CHUNK + j * P, c * CHUNK + (j + 1) * P)
+                nc.tensor.matmul(
+                    out=turned[:, j, :],
+                    lhsT=first_three[b][:, block],
+                    rhs=identity[:],
+                    is_transpose=True,
+                    start=True,
+                    stop=False,
+                )
+                nc.tensor.matmul(
+                    out=turned[:, j, :],
+                    lhsT=fourth[b][:, block],
+                    rhs=identity[:],
+                    is_transpose=True,
+                    start=False,
+                    stop=True,
+                )
+            nc.vector.tensor_reduce(
+                out=sums[:, m * BLOCKS : (m + 1) * BLOCKS], in_=turned[:], axis=AXIS.X, op=ALU.add
+            )
 
         def is_tile(t):
             return 0 <= t < TILES
 
         quantise_x(0)
-        quantise_weight(wk_raw, wk_codes, wk_scales, 0, CHUNKS)
-        for t in range(TILES + VALUE_LAG):
+        quantise_weight(wk_raw, wk_codes, wk_scales, 0, CHUNKS, nc.scalar.copy)
+        for t in range(TILES + VALUE_LAG + SUM_LAG):
             if is_tile(t):
                 key_products(t)
             if is_tile(t - 1):
@@ -233,26 +263,19 @@ def tile_hydraencoderlayer_pa_kernel(tc, x, wk, wv, out):
                 sum_of_squares(t)
             if t < VALUE_LAG:
                 share = CHUNKS // VALUE_LAG
-                quantise_weight(wv_raw, wv_codes, wv_scales, t * share, share)
+                quantise_weight(wv_raw, wv_codes, wv_scales, t * share, share, nc.vector.tensor_copy)
             if is_tile(t - VALUE_LAG):
                 value_stage(t - VALUE_LAG)
             if is_tile(t - 1):
                 invert_norm(t - 1)
-            if t % GROUP == GROUP - 2 and t // GROUP + 1 < GROUPS:
-                quantise_x(t // GROUP + 1)
+            if is_tile(t) and t % TILES_PER_BATCH == 2 and t // TILES_PER_BATCH + 1 < BATCHES:
+                quantise_x(t // TILES_PER_BATCH + 1)
+            if is_tile(t - VALUE_LAG - SUM_LAG):
+                sum_over_tokens(t - VALUE_LAG - SUM_LAG)
 
-        totals = key_banks.tile([P, CHUNK], F32, tag="bank")
-        for c in range(CHUNKS):
-            nc.tensor.matmul(
-                out=totals[:],
-                lhsT=selector[:, CHUNKS - 1 - c : CHUNKS - 1 - c + P],
-                rhs=lane_sums[:, c * CHUNK : (c + 1) * CHUNK],
-                start=(c == 0),
-                stop=(c == CHUNKS - 1),
-            )
-        rows = BATCHES * CHUNKS
-        result = keep.tile([P, CHUNK], F32)
-        nc.scalar.copy(out=result[0:rows, :], in_=totals[0:rows, :])
-        nc.sync.dma_start(
-            out=out.rearrange("b o (c n) -> (b o c) n", n=CHUNK), in_=result[0:rows, :]
-        )
+        rows = BATCHES * CHUNKS * BLOCKS
+        turned_sums = key_banks.tile([P, P], F32, tag="bank")
+        nc.tensor.transpose(turned_sums[:], sums[:], identity[:])
+        result = keep.tile([P, P], F32)
+        nc.vector.tensor_copy(out=result[:], in_=turned_sums[:])
+        nc.sync.dma_start(out=out.rearrange("b o (r p) -> (b o r) p", p=P), in_=result[0:rows, :])

@@ -25,7 +25,7 @@ BLOCKS = CHUNK // P
 TILES_PER_BATCH = TOKENS // P
 TILES = BATCHES * TILES_PER_BATCH
 VALUE_LAG = 2
-SUM_LAG = TILES_PER_BATCH
+SUM_LAG = TILES_PER_BATCH - 1
 
 FLOPS = 2 * 2 * BATCHES * TOKENS * FEATURES * WIDTH
 

from contextlib import ExitStack

import concourse.mybir as mybir
from concourse.masks import make_identity

F32 = mybir.dt.float32
BF16 = mybir.dt.bfloat16
U32 = mybir.dt.uint32
U8 = mybir.dt.uint8
FP8X4 = mybir.dt.float8_e4m3fn_x4
ALU = mybir.AluOpType
ACT = mybir.ActivationFunctionType
AXIS = mybir.AxisListType

P = 128
PACK = 4
BATCHES = 4
TOKENS = 512
FEATURES = 512
WIDTH = 2048
EPS = 1e-12
CHUNK = 512
CHUNKS = WIDTH // CHUNK
BLOCKS = CHUNK // P
TILES_PER_BATCH = TOKENS // P
TILES = BATCHES * TILES_PER_BATCH
VALUE_LAG = 2
SUM_LAG = TILES_PER_BATCH - 1

FLOPS = 2 * 2 * BATCHES * TOKENS * FEATURES * WIDTH


def tile_hydraencoderlayer_pa_kernel(tc, x, wk, wv, out):
    nc = tc.nc
    with ExitStack() as ctx:
        ctx.enter_context(tc.manual_schedule())
        keep = ctx.enter_context(tc.tile_pool(name="keep", bufs=1))
        raw_pool = ctx.enter_context(tc.tile_pool(name="raw", bufs=2 * CHUNKS))
        grouped_pool = ctx.enter_context(tc.tile_pool(name="grouped", bufs=4))
        key_pool = ctx.enter_context(tc.tile_pool(name="keys", bufs=VALUE_LAG + 2))
        square_pool = ctx.enter_context(tc.tile_pool(name="squares", bufs=2))
        norm_pool = ctx.enter_context(tc.tile_pool(name="norms", bufs=VALUE_LAG + 2))
        product_pool = ctx.enter_context(tc.tile_pool(name="products", bufs=2 * CHUNKS))
        batch_pool = ctx.enter_context(tc.tile_pool(name="batch_sums", bufs=2))
        key_banks = ctx.enter_context(tc.psum_pool(name="key_banks", bufs=4))
        value_banks = ctx.enter_context(tc.psum_pool(name="value_banks", bufs=4))

        x_raw = keep.tile([P, BATCHES, TILES_PER_BATCH, FEATURES], BF16)

        def load_x(b):
            nc.sync.dma_start(
                out=x_raw[:, b], in_=x[b].rearrange("(p t) k -> p t k", t=TILES_PER_BATCH)
            )

        def load_weight_chunk(w, c):
            raw = raw_pool.tile([P, PACK, CHUNK], BF16, tag="raw")
            for u in range(2):
                nc.sync.dma_start(
                    out=raw[:, 2 * u : 2 * u + 2, :],
                    in_=w[256 * u : 256 * u + 256, c * CHUNK : (c + 1) * CHUNK].rearrange(
                        "(p e) c -> p e c", e=2
                    ),
                )
            return raw

        load_x(0)
        wk_raw = [load_weight_chunk(wk, c) for c in range(CHUNKS)]
        load_x(1)
        wv_raw = [load_weight_chunk(wv, c) for c in range(CHUNKS)]
        load_x(2)
        load_x(3)

        identity = keep.tile([P, P], F32)
        make_identity(nc, identity[:])
        sums = keep.tile([P, P], F32)
        nc.vector.memset(sums[:], 0.0)
        one = keep.tile([P, 1], F32)
        nc.vector.memset(one[:], 1.0)
        nc.scalar.sqrt(out=one[:], in_=one[:])

        x_codes = keep.tile([P, TILES * P], U32, align_bytes=64)
        x_scales = keep.tile([P, TILES * P], U8, align_bytes=64)
        wk_codes = keep.tile([P, WIDTH], U32, align_bytes=64)
        wk_scales = keep.tile([P, WIDTH], U8, align_bytes=64)
        wv_codes = keep.tile([P, WIDTH], U32, align_bytes=64)
        wv_scales = keep.tile([P, WIDTH], U8, align_bytes=64)

        def quantise_x(b):
            x_words = x_raw[:].bitcast(F32)
            x_grouped = grouped_pool.tile(
                [P, TOKENS, PACK], BF16, tag="x_grouped", bufs=2, align_bytes=64
            )
            grouped_words = x_grouped[:].bitcast(F32)
            for half in range(2):
                flipped = key_banks.tile([P, 2, 2, P], F32, tag="bank")
                for i in range(2):
                    for u in range(2):
                        nc.tensor.transpose(
                            flipped[:, i, u, :],
                            x_words[:, b, 2 * half + i, u * P : (u + 1) * P],
                            identity[:],
                        )
                nc.vector.tensor_copy(
                    out=grouped_words[:, 2 * half * P : 2 * (half + 1) * P, :].rearrange(
                        "p (i k) u -> p i k u", i=2
                    ),
                    in_=flipped[:].rearrange("p i u k -> p i k u"),
                )
            columns = slice(b * TOKENS, (b + 1) * TOKENS)
            nc.vector.quantize_mx(
                out=x_codes[:, columns].bitcast(FP8X4),
                scales=x_scales[:, columns],
                in_=x_grouped[:].rearrange("p k t -> p (k t)"),
            )

        def regroup_weight_chunk(raw, copy):
            grouped = grouped_pool.tile([P, CHUNK, PACK], BF16, tag="w_grouped", align_bytes=64)
            copy(
                out=grouped[:].rearrange("p (c i) t -> p c t i", i=4),
                in_=raw[:].rearrange("p t (c i) -> p c t i", i=4),
            )
            return grouped

        def quantise_weight_chunk(grouped, codes, scales, c):
            columns = slice(c * CHUNK, (c + 1) * CHUNK)
            nc.vector.quantize_mx(
                out=codes[:, columns].bitcast(FP8X4),
                scales=scales[:, columns],
                in_=grouped[:].rearrange("p c t -> p (c t)"),
            )

        def quantise_weight(raws, codes, scales, first, count, odd_copy):
            grouped = [None] * CHUNKS
            for c in range(first, first + count + 1):
                if c < first + count:
                    copy = odd_copy if c % 2 == 1 else nc.vector.tensor_copy
                    grouped[c] = regroup_weight_chunk(raws[c], copy)
                if c > first:
                    quantise_weight_chunk(grouped[c - 1], codes, scales, c - 1)

        keys = [None] * TILES
        norms_squared = [None] * TILES
        norms = [None] * TILES
        inverse_norms = [None] * TILES
        first_three = [None] * BATCHES
        fourth = [None] * BATCHES

        def key_products(t):
            tokens = slice(t * P, (t + 1) * P)
            keys[t] = key_pool.tile([P, WIDTH], F32, name="a_sb", tag="a_sb")
            for c in range(CHUNKS):
                columns = slice(c * CHUNK, (c + 1) * CHUNK)
                a_bank = key_banks.tile([P, CHUNK], F32, tag="bank")
                nc.tensor.matmul_mx(
                    out=a_bank[:],
                    lhsT=x_codes[:, tokens].bitcast(FP8X4),
                    lhsT_scale=x_scales[:, tokens],
                    rhs=wk_codes[:, columns].bitcast(FP8X4),
                    rhs_scale=wk_scales[:, columns],
                    start=True,
                    stop=True,
                )
                if c == 0:
                    nc.vector.tensor_copy(out=keys[t][:, columns], in_=a_bank[:])
                else:
                    nc.scalar.copy(out=keys[t][:, columns], in_=a_bank[:])

        def sum_of_squares(t):
            squares = square_pool.tile([P, WIDTH], BF16, tag="squares")
            norms_squared[t] = norm_pool.tile([P, 1], F32, name="norm_squared", tag="norm_squared")
            nc.scalar.activation(
                out=squares[:], in_=keys[t][:], func=ACT.Square, accum_out=norms_squared[t][:]
            )

        def clamp_and_root(t):
            clamped = norm_pool.tile([P, 1], F32, tag="clamped")
            nc.vector.tensor_scalar_max(out=clamped[:], in0=norms_squared[t][:], scalar1=EPS * EPS)
            norms[t] = norm_pool.tile([P, 1], F32, name="norm", tag="norm")
            nc.scalar.sqrt(out=norms[t][:], in_=clamped[:])

        def invert_norm(t):
            inverse_norms[t] = norm_pool.tile([P, 1], F32, name="inverse_norm", tag="inverse_norm")
            nc.vector.reciprocal(out=inverse_norms[t][:], in_=norms[t][:])

        def value_stage(t):
            b, place = divmod(t, TILES_PER_BATCH)
            tokens = slice(t * P, (t + 1) * P)
            if place == 0:
                first_three[b] = batch_pool.tile([P, WIDTH], F32, name="first_three", tag="first_three")
            if place == TILES_PER_BATCH - 1:
                fourth[b] = batch_pool.tile([P, WIDTH], F32, name="fourth", tag="fourth")
            for c in range(CHUNKS):
                columns = slice(c * CHUNK, (c + 1) * CHUNK)
                v_bank = value_banks.tile([P, CHUNK], F32, tag="bank")
                nc.tensor.matmul_mx(
                    out=v_bank[:],
                    lhsT=x_codes[:, tokens].bitcast(FP8X4),
                    lhsT_scale=x_scales[:, tokens],
                    rhs=wv_codes[:, columns].bitcast(FP8X4),
                    rhs_scale=wv_scales[:, columns],
                    start=True,
                    stop=True,
                )
                if place == 0:
                    product = first_three[b][:, columns]
                elif place == TILES_PER_BATCH - 1:
                    product = fourth[b][:, columns]
                else:
                    product_tile = product_pool.tile([P, CHUNK], F32, tag="product")
                    product = product_tile[:]
                nc.vector.scalar_tensor_tensor(
                    out=product,
                    in0=v_bank[:],
                    scalar=inverse_norms[t][:],
                    in1=keys[t][:, columns],
                    op0=ALU.mult,
                    op1=ALU.mult,
                )
                if 0 < place < TILES_PER_BATCH - 1:
                    nc.gpsimd.tensor_tensor(
                        out=first_three[b][:, columns],
                        in0=first_three[b][:, columns],
                        in1=product,
                        op=ALU.add,
                    )

        def sum_over_tokens(m):
            b, c = divmod(m, CHUNKS)
            turned = value_banks.tile([P, BLOCKS, P], F32, tag="bank")
            for j in range(BLOCKS):
                block = slice(c * CHUNK + j * P, c * CHUNK + (j + 1) * P)
                nc.tensor.matmul(
                    out=turned[:, j, :],
                    lhsT=first_three[b][:, block],
                    rhs=identity[:],
                    is_transpose=True,
                    start=True,
                    stop=False,
                )
                nc.tensor.matmul(
                    out=turned[:, j, :],
                    lhsT=fourth[b][:, block],
                    rhs=identity[:],
                    is_transpose=True,
                    start=False,
                    stop=True,
                )
            nc.vector.tensor_reduce(
                out=sums[:, m * BLOCKS : (m + 1) * BLOCKS], in_=turned[:], axis=AXIS.X, op=ALU.add
            )

        def is_tile(t):
            return 0 <= t < TILES

        quantise_x(0)
        quantise_weight(wk_raw, wk_codes, wk_scales, 0, CHUNKS, nc.scalar.copy)
        for t in range(TILES + VALUE_LAG + SUM_LAG):
            if is_tile(t):
                key_products(t)
            if is_tile(t - 1):
                clamp_and_root(t - 1)
            if is_tile(t):
                sum_of_squares(t)
            if t < VALUE_LAG:
                share = CHUNKS // VALUE_LAG
                quantise_weight(wv_raw, wv_codes, wv_scales, t * share, share, nc.vector.tensor_copy)
            if is_tile(t - VALUE_LAG):
                value_stage(t - VALUE_LAG)
            if is_tile(t - 1):
                invert_norm(t - 1)
            if is_tile(t) and t % TILES_PER_BATCH == 2 and t // TILES_PER_BATCH + 1 < BATCHES:
                quantise_x(t // TILES_PER_BATCH + 1)
            if is_tile(t - VALUE_LAG - SUM_LAG):
                sum_over_tokens(t - VALUE_LAG - SUM_LAG)

        rows = BATCHES * CHUNKS * BLOCKS
        turned_sums = key_banks.tile([P, P], F32, tag="bank")
        nc.tensor.transpose(turned_sums[:], sums[:], identity[:])
        result = keep.tile([P, P], F32)
        nc.vector.tensor_copy(out=result[:], in_=turned_sums[:])
        nc.sync.dma_start(out=out.rearrange("b o (r p) -> (b o r) p", p=P), in_=result[0:rows, :])
